import numpy as np
import ml_dtypes


def mxq(x, axis, fmt="e4m3"):
    dtype, down = {"e4m3": (ml_dtypes.float8_e4m3fn, 7), "e5m2": (ml_dtypes.float8_e5m2, 14)}[fmt]
    v = np.moveaxis(np.asarray(x, np.float32).astype(ml_dtypes.bfloat16).astype(np.float64), axis, -1)
    blocks = v.reshape(v.shape[:-1] + (-1, 32))
    amax = np.abs(blocks).max(-1, keepdims=True)
    byte = np.maximum(np.where(amax > 0, np.frexp(amax)[1] - 1 + 127, 0) - down, 1)
    scale = np.exp2(byte - 127.0)
    codes = (blocks / scale).astype(np.float32).astype(dtype).astype(np.float64)
    return np.moveaxis((codes * scale).reshape(v.shape), -1, axis)


WIDE = False


def mx_kscale(k):
    if not WIDE:
        return np.ones(k)
    levels = np.array([10, -10, 5, -5, 0])
    a = np.random.permutation(np.resize(levels, k // 512 * 4)).reshape(k // 512, 4)
    idx = np.arange(k)
    return np.exp2(a[idx // 512, idx % 128 // 32])


BF16 = ml_dtypes.bfloat16


def bf(x):
    return np.asarray(x, np.float32).astype(BF16)


def f64(x):
    return np.asarray(x).astype(np.float64)


B, S, H, I, R = 4, 32, 1024, 1024, 512
EPS = 1e-05


def rmsnorm(h, w):
    var = np.mean(h * h, axis=-1, keepdims=True)
    return h * (1.0 / np.sqrt(var + EPS)) * w


def silu(v):
    return v / (1.0 + np.exp(-v))


def setup_inputs():
    s, t = mx_kscale(H), mx_kscale(R)
    return {"x": bf(np.random.standard_normal((B, S, H))),
            "residual": bf(np.random.standard_normal((B, S, H))),
            "ln_w": bf((1.0 + 0.1 * np.random.standard_normal(H)) * s),
            "w_gate_v": bf(np.random.standard_normal((H, R)) / np.sqrt(H) / s[:, None] * t),
            "w_gate_u": bf(np.random.standard_normal((R, I)) / np.sqrt(R) / t[:, None]),
            "w_up_v": bf(np.random.standard_normal((H, R)) / np.sqrt(H) / s[:, None] * t),
            "w_up_u": bf(np.random.standard_normal((R, I)) / np.sqrt(R) / t[:, None])}


def reference(x, residual, ln_w, w_gate_v, w_gate_u, w_up_v, w_up_u):
    h = f64(x) + f64(residual)
    n = rmsnorm(h, f64(ln_w))
    nq = mxq(n, 2, "e4m3")
    gate_r = nq @ mxq(f64(w_gate_v), 0, "e4m3")
    up_r = nq @ mxq(f64(w_up_v), 0, "e4m3")
    gate = silu(mxq(gate_r, 2, "e4m3") @ mxq(f64(w_gate_u), 0, "e4m3"))
    up = mxq(up_r, 2, "e4m3") @ mxq(f64(w_up_u), 0, "e4m3")
    return gate * up

@@ -1,0 +1,253 @@
+import concourse.mybir as mybir
+from concourse.masks import make_identity
+
+BF16 = mybir.dt.bfloat16
+F32 = mybir.dt.float32
+U32 = mybir.dt.uint32
+U8 = mybir.dt.uint8
+FP8X4 = mybir.dt.float8_e4m3fn_x4
+ALU = mybir.AluOpType
+ACT = mybir.ActivationFunctionType
+
+P = 128
+PACK = 4
+K_PASS = P * PACK
+H = 1024
+R = 512
+I = 1024
+PASSES = H // K_PASS
+HALVES = I // 512
+EPS = 1e-05
+CHUNK = 512
+RUN = 4
+VECTOR_COLS = 256
+
+FLOPS = 2 * P * (2 * H * R + 2 * R * I)
+
+
+def tile_neuronllamamlp_pa_s_kernel(
+    tc, x, residual, ln_w, w_gate_v, w_gate_u, w_up_v, w_up_u, out
+):
+    nc = tc.nc
+    x_rows = x.flatten_outer_dims()
+    res_rows = residual.flatten_outer_dims()
+    out_rows = out.flatten_outer_dims()
+
+    with tc.tile_pool(name="keep", bufs=1) as keep, tc.psum_pool(
+        name="psum", bufs=1
+    ) as psum, tc.manual_schedule():
+        ident = keep.tile([P, P], F32, name="ident")
+        make_identity(nc, ident[:])
+        neg_half = keep.tile([P, 1], F32, name="neg_half")
+        nc.gpsimd.memset(neg_half[:], -0.5)
+        warm_in = keep.tile([P, 1], F32, name="warm_in")
+        warm_out = keep.tile([P, 1], F32, name="warm_out")
+        nc.vector.memset(warm_in[:], 0.0)
+        nc.scalar.activation(out=warm_out[:], in_=warm_in[:], func=ACT.Silu)
+
+        x_sb = keep.tile([P, PASSES, K_PASS], BF16, name="x_sb")
+        res_sb = keep.tile([P, PASSES, K_PASS], BF16, name="res_sb")
+        for g in range(PASSES):
+            cols = slice(g * K_PASS, (g + 1) * K_PASS)
+            nc.sync.dma_start(out=x_sb[:, g, :], in_=x_rows[:, cols])
+            nc.sync.dma_start(out=res_sb[:, g, :], in_=res_rows[:, cols])
+        ln_sb = keep.tile([P, PASSES, PACK], BF16, name="ln_sb")
+        nc.scalar.dma_start(out=ln_sb[:], in_=ln_w.rearrange("(g p j) -> p g j", p=P, j=PACK))
+
+        chunk_views = []
+        for w in (w_gate_v, w_up_v):
+            for g in range(PASSES):
+                rows = w[g * K_PASS : (g + 1) * K_PASS, :]
+                chunk_views.append(rows.rearrange("(p j) r -> p j r", j=PACK))
+        for half in range(HALVES):
+            for w in (w_gate_u, w_up_u):
+                cols = w[:, half * CHUNK : (half + 1) * CHUNK]
+                chunk_views.append(cols.rearrange("(j p) i -> p j i", p=P))
+
+        raws, groupeds, codes, scales = [], [], [], []
+        for c, view in enumerate(chunk_views):
+            raws.append(keep.tile([P, PACK, CHUNK], BF16, name="raw%d" % c))
+            groupeds.append(keep.tile([P, CHUNK, PACK], BF16, name="grouped%d" % c, align_bytes=64))
+            codes.append(keep.tile([P, CHUNK], U32, name="codes%d" % c, align_bytes=64))
+            scales.append(keep.tile([P, CHUNK], U8, name="scales%d" % c, align_bytes=64))
+            nc.sync.dma_start(out=raws[c][:], in_=view)
+
+        def regroup(c):
+            for copy, cols in (
+                (nc.vector.tensor_copy, slice(0, VECTOR_COLS)),
+                (nc.scalar.copy, slice(VECTOR_COLS, CHUNK)),
+            ):
+                copy(
+                    out=groupeds[c][:, cols, :].rearrange("p (w i) j -> p w j i", i=RUN),
+                    in_=raws[c][:, :, cols].rearrange("p j (w i) -> p w j i", i=RUN),
+                )
+
+        def quantise(c):
+            nc.vector.quantize_mx(
+                out=codes[c][:].bitcast(FP8X4),
+                scales=scales[c][:],
+                in_=groupeds[c][:].rearrange("p w j -> p (w j)"),
+            )
+
+        h_perm = keep.tile([P, PASSES, PACK, P], F32, name="h_perm")
+        h_norm = keep.tile([P, PASSES, PACK, P], F32, name="h_norm")
+        squares = keep.tile([P, PASSES, K_PASS], BF16, name="squares")
+        mean_parts = keep.tile([P, PASSES], F32, name="mean_parts")
+        mean_sq = keep.tile([P, 1], F32, name="mean_sq")
+        rstd = keep.tile([P, 1], F32, name="rstd")
+        n_grouped = keep.tile([P, PASSES, P, PACK], BF16, name="n_grouped", align_bytes=64)
+        n_codes = keep.tile([P, PASSES, P], U32, name="n_codes", align_bytes=64)
+        n_scales = keep.tile([P, PASSES, P], U8, name="n_scales", align_bytes=64)
+
+        def add_and_square(g):
+            nc.vector.tensor_tensor(
+                out=h_perm[:, g],
+                in0=x_sb[:, g, :].rearrange("t (p j) -> t j p", j=PACK),
+                in1=res_sb[:, g, :].rearrange("t (p j) -> t j p", j=PACK),
+                op=ALU.add,
+            )
+            nc.scalar.activation(
+                out=squares[:, g, :],
+                in_=h_perm[:, g].rearrange("t j p -> t (j p)"),
+                func=ACT.Square,
+                scale=H**-0.5,
+                accum_out=mean_parts[:, g : g + 1],
+            )
+
+        def reciprocal_std():
+            nc.gpsimd.tensor_scalar(
+                out=mean_sq[:],
+                in0=mean_parts[:, 0:1],
+                scalar1=mean_parts[:, 1:2],
+                scalar2=EPS,
+                op0=ALU.add,
+                op1=ALU.add,
+            )
+            nc.gpsimd.tensor_tensor(out=rstd[:], in0=mean_sq[:], in1=neg_half[:], op=ALU.pow)
+
+        hT = [psum.tile([P, PACK, P], F32, name="hT%d" % g) for g in range(PASSES)]
+
+        def normalise_and_transpose(g):
+            nc.scalar.activation(
+                out=h_norm[:, g].rearrange("t j p -> t (j p)"),
+                in_=h_perm[:, g].rearrange("t j p -> t (j p)"),
+                func=ACT.Copy,
+                scale=rstd[:],
+            )
+            for j in range(PACK):
+                nc.tensor.transpose(hT[g][:, j, :], h_norm[:, g, j, :], ident[:])
+
+        def apply_gain(g):
+            nc.vector.tensor_tensor(
+                out=n_grouped[:, g],
+                in0=hT[g][:].rearrange("p j t -> p t j"),
+                in1=ln_sb[:, g, :].unsqueeze(1).to_broadcast([P, P, PACK]),
+                op=ALU.mult,
+            )
+
+        def quantise_n():
+            nc.vector.quantize_mx(
+                out=n_codes[:].rearrange("p g t -> p (g t)").bitcast(FP8X4),
+                scales=n_scales[:].rearrange("p g t -> p (g t)"),
+                in_=n_grouped[:].rearrange("p g t j -> p (g t j)"),
+            )
+
+        rT = [psum.tile([P, PACK, P], F32, name="rT%d" % m) for m in range(2)]
+        r_grouped = [
+            keep.tile([P, P, PACK], BF16, name="r_grouped%d" % m, align_bytes=64) for m in range(2)
+        ]
+        r_codes = [keep.tile([P, P], U32, name="r_codes%d" % m, align_bytes=64) for m in range(2)]
+        r_scales = [keep.tile([P, P], U8, name="r_scales%d" % m, align_bytes=64) for m in range(2)]
+
+        def first_contraction(m):
+            for b in range(PACK):
+                for g in range(PASSES):
+                    c = m * PASSES + g
+                    nc.tensor.matmul_mx(
+                        out=rT[m][:, b, :],
+                        lhsT=codes[c][:, b * P : (b + 1) * P].bitcast(FP8X4),
+                        lhsT_scale=scales[c][:, b * P : (b + 1) * P],
+                        rhs=n_codes[:, g, :].bitcast(FP8X4),
+                        rhs_scale=n_scales[:, g, :],
+                        start=(g == 0),
+                        stop=(g == PASSES - 1),
+                    )
+
+        def round_r(m):
+            nc.scalar.copy(out=r_grouped[m][:], in_=rT[m][:].rearrange("p b t -> p t b"))
+
+        def quantise_r(m):
+            nc.vector.quantize_mx(
+                out=r_codes[m][:].bitcast(FP8X4),
+                scales=r_scales[m][:],
+                in_=r_grouped[m][:].rearrange("p t b -> p (t b)"),
+            )
+
+        products = [
+            [psum.tile([P, CHUNK], F32, name="product%d_%d" % (m, half)) for half in range(HALVES)]
+            for m in range(2)
+        ]
+        gates = [keep.tile([P, CHUNK], F32, name="gate%d" % half) for half in range(HALVES)]
+        results = [keep.tile([P, CHUNK], F32, name="result%d" % half) for half in range(HALVES)]
+
+        def second_contraction(m, half):
+            c = 2 * PASSES + half * 2 + m
+            nc.tensor.matmul_mx(
+                out=products[m][half][:],
+                lhsT=r_codes[m][:].bitcast(FP8X4),
+                lhsT_scale=r_scales[m][:],
+                rhs=codes[c][:].bitcast(FP8X4),
+                rhs_scale=scales[c][:],
+                start=True,
+                stop=True,
+            )
+
+        def silu_gate(half):
+            nc.scalar.activation(out=gates[half][:], in_=products[0][half][:], func=ACT.Silu)
+
+        def multiply_and_store(half):
+            nc.vector.tensor_tensor(
+                out=results[half][:], in0=gates[half][:], in1=products[1][half][:], op=ALU.mult
+            )
+            nc.sync.dma_start(
+                out=out_rows[:, half * CHUNK : (half + 1) * CHUNK], in_=results[half][:]
+            )
+
+        add_and_square(0)
+        add_and_square(1)
+        reciprocal_std()
+        regroup(0)
+        normalise_and_transpose(0)
+        normalise_and_transpose(1)
+        regroup(1)
+        quantise(0)
+        apply_gain(0)
+        apply_gain(1)
+        regroup(2)
+        quantise_n()
+        quantise(1)
+        regroup(3)
+        quantise(2)
+        first_contraction(0)
+        regroup(4)
+        quantise(3)
+        first_contraction(1)
+        round_r(0)
+        regroup(5)
+        quantise(4)
+        quantise_r(0)
+        regroup(6)
+        round_r(1)
+        quantise(5)
+        quantise_r(1)
+        second_contraction(0, 0)
+        second_contraction(1, 0)
+        regroup(7)
+        silu_gate(0)
+        quantise(6)
+        second_contraction(0, 1)
+        quantise(7)
+        multiply_and_store(0)
+        silu_gate(1)
+        second_contraction(1, 1)
+        multiply_and_store(1)

@@ -16,11 +16,12 @@ H = 1024
 R = 512
 I = 1024
 PASSES = H // K_PASS
-HALVES = I // 512
 EPS = 1e-05
 CHUNK = 512
+SHARE = CHUNK // 2
+VECTOR, SCALAR = 0, 1
 RUN = 4
-VECTOR_COLS = 256
+GATE, UP = 0, 1
 
 FLOPS = 2 * P * (2 * H * R + 2 * R * I)
 
@@ -59,45 +60,66 @@ def tile_neuronllamamlp_pa_s_kernel(
             for g in range(PASSES):
                 rows = w[g * K_PASS : (g + 1) * K_PASS, :]
                 chunk_views.append(rows.rearrange("(p j) r -> p j r", j=PACK))
-        for half in range(HALVES):
-            for w in (w_gate_u, w_up_u):
+        for w in (w_gate_u, w_up_u):
+            for half in range(I // CHUNK):
                 cols = w[:, half * CHUNK : (half + 1) * CHUNK]
                 chunk_views.append(cols.rearrange("(j p) i -> p j i", p=P))
 
         raws, groupeds, codes, scales = [], [], [], []
         for c, view in enumerate(chunk_views):
             raws.append(keep.tile([P, PACK, CHUNK], BF16, name="raw%d" % c))
-            groupeds.append(keep.tile([P, CHUNK, PACK], BF16, name="grouped%d" % c, align_bytes=64))
-            codes.append(keep.tile([P, CHUNK], U32, name="codes%d" % c, align_bytes=64))
-            scales.append(keep.tile([P, CHUNK], U8, name="scales%d" % c, align_bytes=64))
             nc.sync.dma_start(out=raws[c][:], in_=view)
-
-        def regroup(c):
-            for copy, cols in (
-                (nc.vector.tensor_copy, slice(0, VECTOR_COLS)),
-                (nc.scalar.copy, slice(VECTOR_COLS, CHUNK)),
-            ):
-                copy(
-                    out=groupeds[c][:, cols, :].rearrange("p (w i) j -> p w j i", i=RUN),
-                    in_=raws[c][:, :, cols].rearrange("p j (w i) -> p w j i", i=RUN),
-                )
-
-        def quantise(c):
-            nc.vector.quantize_mx(
-                out=codes[c][:].bitcast(FP8X4),
-                scales=scales[c][:],
-                in_=groupeds[c][:].rearrange("p w j -> p (w j)"),
+            groupeds.append(
+                [
+                    keep.tile([P, SHARE, PACK], BF16, name="grouped%d_%d" % (c, s), align_bytes=64)
+                    for s in (VECTOR, SCALAR)
+                ]
+            )
+            codes.append(
+                [
+                    keep.tile([P, SHARE], U32, name="codes%d_%d" % (c, s), align_bytes=64)
+                    for s in (VECTOR, SCALAR)
+                ]
+            )
+            scales.append(
+                [
+                    keep.tile([P, SHARE], U8, name="scales%d_%d" % (c, s), align_bytes=64)
+                    for s in (VECTOR, SCALAR)
+                ]
             )
 
+        def regroup(c):
+            for s, copy in ((VECTOR, nc.vector.tensor_copy), (SCALAR, nc.scalar.copy)):
+                copy(
+                    out=groupeds[c][s][:].rearrange("p (w i) j -> p w j i", i=RUN),
+                    in_=raws[c][:, :, s * SHARE : (s + 1) * SHARE].rearrange(
+                        "p j (w i) -> p w j i", i=RUN
+                    ),
+                )
+
+        def quantise(c, s):
+            nc.vector.quantize_mx(
+                out=codes[c][s][:].bitcast(FP8X4),
+                scales=scales[c][s][:],
+                in_=groupeds[c][s][:].rearrange("p w j -> p (w j)"),
+            )
+
+        def take_chunk(c):
+            regroup(c)
+            if c > 0:
+                quantise(c - 1, SCALAR)
+            quantise(c, VECTOR)
+
         h_perm = keep.tile([P, PASSES, PACK, P], F32, name="h_perm")
-        h_norm = keep.tile([P, PASSES, PACK, P], F32, name="h_norm")
         squares = keep.tile([P, PASSES, K_PASS], BF16, name="squares")
         mean_parts = keep.tile([P, PASSES], F32, name="mean_parts")
         mean_sq = keep.tile([P, 1], F32, name="mean_sq")
         rstd = keep.tile([P, 1], F32, name="rstd")
+        rstd_diag = keep.tile([P, P], F32, name="rstd_diag")
         n_grouped = keep.tile([P, PASSES, P, PACK], BF16, name="n_grouped", align_bytes=64)
         n_codes = keep.tile([P, PASSES, P], U32, name="n_codes", align_bytes=64)
         n_scales = keep.tile([P, PASSES, P], U8, name="n_scales", align_bytes=64)
+        hT = [psum.tile([P, PACK, P], F32, name="hT%d" % g, tag="bank%d" % g) for g in range(PASSES)]
 
         def add_and_square(g):
             nc.vector.tensor_tensor(
@@ -124,18 +146,24 @@ def tile_neuronllamamlp_pa_s_kernel(
                 op1=ALU.add,
             )
             nc.gpsimd.tensor_tensor(out=rstd[:], in0=mean_sq[:], in1=neg_half[:], op=ALU.pow)
-
-        hT = [psum.tile([P, PACK, P], F32, name="hT%d" % g) for g in range(PASSES)]
-
-        def normalise_and_transpose(g):
-            nc.scalar.activation(
-                out=h_norm[:, g].rearrange("t j p -> t (j p)"),
-                in_=h_perm[:, g].rearrange("t j p -> t (j p)"),
-                func=ACT.Copy,
-                scale=rstd[:],
+            nc.gpsimd.tensor_scalar(
+                out=rstd_diag[:],
+                in0=ident[:],
+                scalar1=rstd[:],
+                scalar2=0.0,
+                op0=ALU.mult,
+                op1=ALU.add,
             )
+
+        def normalise_transposed(g):
             for j in range(PACK):
-                nc.tensor.transpose(hT[g][:, j, :], h_norm[:, g, j, :], ident[:])
+                nc.tensor.matmul(
+                    out=hT[g][:, j, :],
+                    lhsT=h_perm[:, g, j, :],
+                    rhs=rstd_diag[:],
+                    start=True,
+                    stop=True,
+                )
 
         def apply_gain(g):
             nc.vector.tensor_tensor(
@@ -152,21 +180,31 @@ def tile_neuronllamamlp_pa_s_kernel(
                 in_=n_grouped[:].rearrange("p g t j -> p (g t j)"),
             )
 
-        rT = [psum.tile([P, PACK, P], F32, name="rT%d" % m) for m in range(2)]
-        r_grouped = [
-            keep.tile([P, P, PACK], BF16, name="r_grouped%d" % m, align_bytes=64) for m in range(2)
+        rT = [
+            psum.tile([P, PACK, P], F32, name="rT%d" % m, tag="bank%d" % (2 + m))
+            for m in (GATE, UP)
         ]
-        r_codes = [keep.tile([P, P], U32, name="r_codes%d" % m, align_bytes=64) for m in range(2)]
-        r_scales = [keep.tile([P, P], U8, name="r_scales%d" % m, align_bytes=64) for m in range(2)]
+        r_grouped = [
+            keep.tile([P, P, PACK], BF16, name="r_grouped%d" % m, align_bytes=64)
+            for m in (GATE, UP)
+        ]
+        r_codes = [
+            keep.tile([P, P], U32, name="r_codes%d" % m, align_bytes=64) for m in (GATE, UP)
+        ]
+        r_scales = [
+            keep.tile([P, P], U8, name="r_scales%d" % m, align_bytes=64) for m in (GATE, UP)
+        ]
 
         def first_contraction(m):
             for b in range(PACK):
+                s = b * P // SHARE
+                cols = slice(b * P - s * SHARE, (b + 1) * P - s * SHARE)
                 for g in range(PASSES):
                     c = m * PASSES + g
                     nc.tensor.matmul_mx(
                         out=rT[m][:, b, :],
-                        lhsT=codes[c][:, b * P : (b + 1) * P].bitcast(FP8X4),
-                        lhsT_scale=scales[c][:, b * P : (b + 1) * P],
+                        lhsT=codes[c][s][:, cols].bitcast(FP8X4),
+                        lhsT_scale=scales[c][s][:, cols],
                         rhs=n_codes[:, g, :].bitcast(FP8X4),
                         rhs_scale=n_scales[:, g, :],
                         start=(g == 0),
@@ -183,71 +221,67 @@ def tile_neuronllamamlp_pa_s_kernel(
                 in_=r_grouped[m][:].rearrange("p t b -> p (t b)"),
             )
 
-        products = [
-            [psum.tile([P, CHUNK], F32, name="product%d_%d" % (m, half)) for half in range(HALVES)]
-            for m in range(2)
+        quarters = I // SHARE
+        gate_products = [
+            psum.tile([P, SHARE], F32, name="gate_product%d" % q, tag="bank%d" % (4 + q))
+            for q in range(quarters)
         ]
-        gates = [keep.tile([P, CHUNK], F32, name="gate%d" % half) for half in range(HALVES)]
-        results = [keep.tile([P, CHUNK], F32, name="result%d" % half) for half in range(HALVES)]
+        gates = [keep.tile([P, SHARE], F32, name="gate%d" % q) for q in range(quarters)]
+        results = [keep.tile([P, SHARE], F32, name="result%d" % q) for q in range(quarters)]
 
-        def second_contraction(m, half):
-            c = 2 * PASSES + half * 2 + m
+        def second_contraction(m, q, product):
+            c = 2 * PASSES + m * (I // CHUNK) + q // 2
+            s = q % 2
             nc.tensor.matmul_mx(
-                out=products[m][half][:],
+                out=product[:],
                 lhsT=r_codes[m][:].bitcast(FP8X4),
                 lhsT_scale=r_scales[m][:],
-                rhs=codes[c][:].bitcast(FP8X4),
-                rhs_scale=scales[c][:],
+                rhs=codes[c][s][:].bitcast(FP8X4),
+                rhs_scale=scales[c][s][:],
                 start=True,
                 stop=True,
             )
 
-        def silu_gate(half):
-            nc.scalar.activation(out=gates[half][:], in_=products[0][half][:], func=ACT.Silu)
+        def gate_quarter(q):
+            second_contraction(GATE, q, gate_products[q])
+            nc.scalar.activation(out=gates[q][:], in_=gate_products[q][:], func=ACT.Silu)
 
-        def multiply_and_store(half):
+        def finish_quarter(q):
+            up_product = psum.tile([P, SHARE], F32, name="up_product%d" % q, tag="bank%d" % q)
+            second_contraction(UP, q, up_product)
             nc.vector.tensor_tensor(
-                out=results[half][:], in0=gates[half][:], in1=products[1][half][:], op=ALU.mult
+                out=results[q][:], in0=gates[q][:], in1=up_product[:], op=ALU.mult
             )
-            nc.sync.dma_start(
-                out=out_rows[:, half * CHUNK : (half + 1) * CHUNK], in_=results[half][:]
-            )
+            nc.sync.dma_start(out=out_rows[:, q * SHARE : (q + 1) * SHARE], in_=results[q][:])
 
         add_and_square(0)
         add_and_square(1)
         reciprocal_std()
-        regroup(0)
-        normalise_and_transpose(0)
-        normalise_and_transpose(1)
-        regroup(1)
-        quantise(0)
+        normalise_transposed(0)
+        normalise_transposed(1)
+        take_chunk(0)
+        take_chunk(1)
+        take_chunk(2)
         apply_gain(0)
+        take_chunk(3)
         apply_gain(1)
-        regroup(2)
         quantise_n()
-        quantise(1)
-        regroup(3)
-        quantise(2)
-        first_contraction(0)
+        quantise(3, SCALAR)
+        first_contraction(GATE)
+        first_contraction(UP)
         regroup(4)
-        quantise(3)
-        first_contraction(1)
-        round_r(0)
-        regroup(5)
-        quantise(4)
-        quantise_r(0)
+        quantise(4, VECTOR)
+        take_chunk(5)
         regroup(6)
-        round_r(1)
-        quantise(5)
-        quantise_r(1)
-        second_contraction(0, 0)
-        second_contraction(1, 0)
-        regroup(7)
-        silu_gate(0)
-        quantise(6)
-        second_contraction(0, 1)
-        quantise(7)
-        multiply_and_store(0)
-        silu_gate(1)
-        second_contraction(1, 1)
-        multiply_and_store(1)
+        round_r(GATE)
+        round_r(UP)
+        quantise(5, SCALAR)
+        quantise_r(GATE)
+        quantise(6, VECTOR)
+        quantise_r(UP)
+        take_chunk(7)
+        for q in range(quarters):
+            gate_quarter(q)
+        quantise(7, SCALAR)
+        for q in range(quarters):
+            finish_quarter(q)

@@ -115,7 +115,7 @@ def tile_neuronllamamlp_pa_s_kernel(
         mean_parts = keep.tile([P, PASSES], F32, name="mean_parts")
         mean_sq = keep.tile([P, 1], F32, name="mean_sq")
         rstd = keep.tile([P, 1], F32, name="rstd")
-        rstd_diag = keep.tile([P, P], F32, name="rstd_diag")
+        h_norm = keep.tile([P, PASSES, PACK, P], F32, name="h_norm")
         n_grouped = keep.tile([P, PASSES, P, PACK], BF16, name="n_grouped", align_bytes=64)
         n_codes = keep.tile([P, PASSES, P], U32, name="n_codes", align_bytes=64)
         n_scales = keep.tile([P, PASSES, P], U8, name="n_scales", align_bytes=64)
@@ -146,24 +146,16 @@ def tile_neuronllamamlp_pa_s_kernel(
                 op1=ALU.add,
             )
             nc.gpsimd.tensor_tensor(out=rstd[:], in0=mean_sq[:], in1=neg_half[:], op=ALU.pow)
-            nc.gpsimd.tensor_scalar(
-                out=rstd_diag[:],
-                in0=ident[:],
-                scalar1=rstd[:],
-                scalar2=0.0,
-                op0=ALU.mult,
-                op1=ALU.add,
-            )
 
         def normalise_transposed(g):
+            nc.scalar.activation(
+                out=h_norm[:, g].rearrange("t j p -> t (j p)"),
+                in_=h_perm[:, g].rearrange("t j p -> t (j p)"),
+                func=ACT.Copy,
+                scale=rstd[:],
+            )
             for j in range(PACK):
-                nc.tensor.matmul(
-                    out=hT[g][:, j, :],
-                    lhsT=h_perm[:, g, j, :],
-                    rhs=rstd_diag[:],
-                    start=True,
-                    stop=True,
-                )
+                nc.tensor.transpose(hT[g][:, j, :], h_norm[:, g, j, :], ident[:])
 
         def apply_gain(g):
             nc.vector.tensor_tensor(
@@ -257,9 +249,9 @@ def tile_neuronllamamlp_pa_s_kernel(
         add_and_square(0)
         add_and_square(1)
         reciprocal_std()
+        take_chunk(0)
         normalise_transposed(0)
         normalise_transposed(1)
-        take_chunk(0)
         take_chunk(1)
         take_chunk(2)
         apply_gain(0)

@@ -16,11 +16,11 @@ H = 1024
 R = 512
 I = 1024
 PASSES = H // K_PASS
+HALVES = I // 512
 EPS = 1e-05
 CHUNK = 512
-SHARE = CHUNK // 2
-VECTOR, SCALAR = 0, 1
 RUN = 4
+VECTOR_COLS = 256
 GATE, UP = 0, 1
 
 FLOPS = 2 * P * (2 * H * R + 2 * R * I)
@@ -37,15 +37,6 @@ def tile_neuronllamamlp_pa_s_kernel(
     with tc.tile_pool(name="keep", bufs=1) as keep, tc.psum_pool(
         name="psum", bufs=1
     ) as psum, tc.manual_schedule():
-        ident = keep.tile([P, P], F32, name="ident")
-        make_identity(nc, ident[:])
-        neg_half = keep.tile([P, 1], F32, name="neg_half")
-        nc.gpsimd.memset(neg_half[:], -0.5)
-        warm_in = keep.tile([P, 1], F32, name="warm_in")
-        warm_out = keep.tile([P, 1], F32, name="warm_out")
-        nc.vector.memset(warm_in[:], 0.0)
-        nc.scalar.activation(out=warm_out[:], in_=warm_in[:], func=ACT.Silu)
-
         x_sb = keep.tile([P, PASSES, K_PASS], BF16, name="x_sb")
         res_sb = keep.tile([P, PASSES, K_PASS], BF16, name="res_sb")
         for g in range(PASSES):
@@ -61,67 +52,59 @@ def tile_neuronllamamlp_pa_s_kernel(
                 rows = w[g * K_PASS : (g + 1) * K_PASS, :]
                 chunk_views.append(rows.rearrange("(p j) r -> p j r", j=PACK))
         for w in (w_gate_u, w_up_u):
-            for half in range(I // CHUNK):
+            for half in range(HALVES):
                 cols = w[:, half * CHUNK : (half + 1) * CHUNK]
                 chunk_views.append(cols.rearrange("(j p) i -> p j i", p=P))
 
         raws, groupeds, codes, scales = [], [], [], []
         for c, view in enumerate(chunk_views):
             raws.append(keep.tile([P, PACK, CHUNK], BF16, name="raw%d" % c))
+            groupeds.append(keep.tile([P, CHUNK, PACK], BF16, name="grouped%d" % c, align_bytes=64))
+            codes.append(keep.tile([P, CHUNK], U32, name="codes%d" % c, align_bytes=64))
+            scales.append(keep.tile([P, CHUNK], U8, name="scales%d" % c, align_bytes=64))
             nc.sync.dma_start(out=raws[c][:], in_=view)
-            groupeds.append(
-                [
-                    keep.tile([P, SHARE, PACK], BF16, name="grouped%d_%d" % (c, s), align_bytes=64)
-                    for s in (VECTOR, SCALAR)
-                ]
-            )
-            codes.append(
-                [
-                    keep.tile([P, SHARE], U32, name="codes%d_%d" % (c, s), align_bytes=64)
-                    for s in (VECTOR, SCALAR)
-                ]
-            )
-            scales.append(
-                [
-                    keep.tile([P, SHARE], U8, name="scales%d_%d" % (c, s), align_bytes=64)
-                    for s in (VECTOR, SCALAR)
-                ]
+
+        ident = keep.tile([P, P], F32, name="ident")
+        make_identity(nc, ident[:])
+        neg_half = keep.tile([P, 1], F32, name="neg_half")
+        nc.gpsimd.memset(neg_half[:], -0.5)
+        warm_in = keep.tile([P, 1], F32, name="warm_in")
+        warm_out = keep.tile([P, 1], F32, name="warm_out")
+        nc.vector.memset(warm_in[:], 0.0)
+        nc.scalar.activation(out=warm_out[:], in_=warm_in[:], func=ACT.Silu)
+        ln_f32 = keep.tile([P, PASSES, PACK], F32, name="ln_f32")
+        nc.gpsimd.tensor_copy(out=ln_f32[:], in_=ln_sb[:])
+
+        def regroup_part(copy, c, cols):
+            copy(
+                out=groupeds[c][:, cols, :].rearrange("p (w i) j -> p w j i", i=RUN),
+                in_=raws[c][:, :, cols].rearrange("p j (w i) -> p w j i", i=RUN),
             )
 
         def regroup(c):
-            for s, copy in ((VECTOR, nc.vector.tensor_copy), (SCALAR, nc.scalar.copy)):
-                copy(
-                    out=groupeds[c][s][:].rearrange("p (w i) j -> p w j i", i=RUN),
-                    in_=raws[c][:, :, s * SHARE : (s + 1) * SHARE].rearrange(
-                        "p j (w i) -> p w j i", i=RUN
-                    ),
-                )
+            regroup_part(nc.vector.tensor_copy, c, slice(0, VECTOR_COLS))
+            regroup_part(nc.scalar.copy, c, slice(VECTOR_COLS, CHUNK))
 
-        def quantise(c, s):
+        def quantise(c):
             nc.vector.quantize_mx(
-                out=codes[c][s][:].bitcast(FP8X4),
-                scales=scales[c][s][:],
-                in_=groupeds[c][s][:].rearrange("p w j -> p (w j)"),
+                out=codes[c][:].bitcast(FP8X4),
+                scales=scales[c][:],
+                in_=groupeds[c][:].rearrange("p w j -> p (w j)"),
             )
-
-        def take_chunk(c):
-            regroup(c)
-            if c > 0:
-                quantise(c - 1, SCALAR)
-            quantise(c, VECTOR)
 
         h_perm = keep.tile([P, PASSES, PACK, P], F32, name="h_perm")
         squares = keep.tile([P, PASSES, K_PASS], BF16, name="squares")
         mean_parts = keep.tile([P, PASSES], F32, name="mean_parts")
         mean_sq = keep.tile([P, 1], F32, name="mean_sq")
         rstd = keep.tile([P, 1], F32, name="rstd")
-        h_norm = keep.tile([P, PASSES, PACK, P], F32, name="h_norm")
+        gained = keep.tile([P, PASSES, PACK, P], F32, name="gained")
         n_grouped = keep.tile([P, PASSES, P, PACK], BF16, name="n_grouped", align_bytes=64)
         n_codes = keep.tile([P, PASSES, P], U32, name="n_codes", align_bytes=64)
         n_scales = keep.tile([P, PASSES, P], U8, name="n_scales", align_bytes=64)
         hT = [psum.tile([P, PACK, P], F32, name="hT%d" % g, tag="bank%d" % g) for g in range(PASSES)]
+        rstd_rows = psum.tile([P, P], F32, name="rstd_rows", tag="bank2")
 
-        def add_and_square(g):
+        def add_square_transpose(g):
             nc.vector.tensor_tensor(
                 out=h_perm[:, g],
                 in0=x_sb[:, g, :].rearrange("t (p j) -> t j p", j=PACK),
@@ -135,6 +118,8 @@ def tile_neuronllamamlp_pa_s_kernel(
                 scale=H**-0.5,
                 accum_out=mean_parts[:, g : g + 1],
             )
+            for j in range(PACK):
+                nc.tensor.transpose(hT[g][:, j, :], h_perm[:, g, j, :], ident[:])
 
         def reciprocal_std():
             nc.gpsimd.tensor_scalar(
@@ -146,22 +131,22 @@ def tile_neuronllamamlp_pa_s_kernel(
                 op1=ALU.add,
             )
             nc.gpsimd.tensor_tensor(out=rstd[:], in0=mean_sq[:], in1=neg_half[:], op=ALU.pow)
-
-        def normalise_transposed(g):
-            nc.scalar.activation(
-                out=h_norm[:, g].rearrange("t j p -> t (j p)"),
-                in_=h_perm[:, g].rearrange("t j p -> t (j p)"),
-                func=ACT.Copy,
-                scale=rstd[:],
-            )
-            for j in range(PACK):
-                nc.tensor.transpose(hT[g][:, j, :], h_norm[:, g, j, :], ident[:])
+            nc.tensor.transpose(rstd_rows[:], rstd[:].to_broadcast([P, P]), ident[:])
 
         def apply_gain(g):
+            for j in range(PACK):
+                nc.scalar.activation(
+                    out=gained[:, g, j, :],
+                    in_=hT[g][:, j, :],
+                    func=ACT.Copy,
+                    scale=ln_f32[:, g, j : j + 1],
+                )
+
+        def normalise(g):
             nc.vector.tensor_tensor(
                 out=n_grouped[:, g],
-                in0=hT[g][:].rearrange("p j t -> p t j"),
-                in1=ln_sb[:, g, :].unsqueeze(1).to_broadcast([P, P, PACK]),
+                in0=gained[:, g].rearrange("p j t -> p t j"),
+                in1=rstd_rows[:].unsqueeze(2).to_broadcast([P, P, PACK]),
                 op=ALU.mult,
             )
 
@@ -173,7 +158,7 @@ def tile_neuronllamamlp_pa_s_kernel(
             )
 
         rT = [
-            psum.tile([P, PACK, P], F32, name="rT%d" % m, tag="bank%d" % (2 + m))
+            psum.tile([P, PACK, P], F32, name="rT%d" % m, tag="bank%d" % (3 + m))
             for m in (GATE, UP)
         ]
         r_grouped = [
@@ -189,14 +174,12 @@ def tile_neuronllamamlp_pa_s_kernel(
 
         def first_contraction(m):
             for b in range(PACK):
-                s = b * P // SHARE
-                cols = slice(b * P - s * SHARE, (b + 1) * P - s * SHARE)
                 for g in range(PASSES):
                     c = m * PASSES + g
                     nc.tensor.matmul_mx(
                         out=rT[m][:, b, :],
-                        lhsT=codes[c][s][:, cols].bitcast(FP8X4),
-                        lhsT_scale=scales[c][s][:, cols],
+                        lhsT=codes[c][:, b * P : (b + 1) * P].bitcast(FP8X4),
+                        lhsT_scale=scales[c][:, b * P : (b + 1) * P],
                         rhs=n_codes[:, g, :].bitcast(FP8X4),
                         rhs_scale=n_scales[:, g, :],
                         start=(g == 0),
@@ -213,67 +196,79 @@ def tile_neuronllamamlp_pa_s_kernel(
                 in_=r_grouped[m][:].rearrange("p t b -> p (t b)"),
             )
 
-        quarters = I // SHARE
-        gate_products = [
-            psum.tile([P, SHARE], F32, name="gate_product%d" % q, tag="bank%d" % (4 + q))
-            for q in range(quarters)
+        products = [
+            [
+                psum.tile(
+                    [P, CHUNK],
+                    F32,
+                    name="product%d_%d" % (m, half),
+                    tag="bank%d" % ((5 + m * HALVES + half) % 8),
+                )
+                for half in range(HALVES)
+            ]
+            for m in (GATE, UP)
         ]
-        gates = [keep.tile([P, SHARE], F32, name="gate%d" % q) for q in range(quarters)]
-        results = [keep.tile([P, SHARE], F32, name="result%d" % q) for q in range(quarters)]
+        gates = [keep.tile([P, CHUNK], F32, name="gate%d" % half) for half in range(HALVES)]
+        results = [keep.tile([P, CHUNK], F32, name="result%d" % half) for half in range(HALVES)]
 
-        def second_contraction(m, q, product):
-            c = 2 * PASSES + m * (I // CHUNK) + q // 2
-            s = q % 2
+        def second_contraction(m, half):
+            c = 2 * PASSES + m * HALVES + half
             nc.tensor.matmul_mx(
-                out=product[:],
+                out=products[m][half][:],
                 lhsT=r_codes[m][:].bitcast(FP8X4),
                 lhsT_scale=r_scales[m][:],
-                rhs=codes[c][s][:].bitcast(FP8X4),
-                rhs_scale=scales[c][s][:],
+                rhs=codes[c][:].bitcast(FP8X4),
+                rhs_scale=scales[c][:],
                 start=True,
                 stop=True,
             )
 
-        def gate_quarter(q):
-            second_contraction(GATE, q, gate_products[q])
-            nc.scalar.activation(out=gates[q][:], in_=gate_products[q][:], func=ACT.Silu)
+        def silu_gate(half):
+            nc.scalar.activation(out=gates[half][:], in_=products[GATE][half][:], func=ACT.Silu)
 
-        def finish_quarter(q):
-            up_product = psum.tile([P, SHARE], F32, name="up_product%d" % q, tag="bank%d" % q)
-            second_contraction(UP, q, up_product)
+        def multiply_and_store(half):
             nc.vector.tensor_tensor(
-                out=results[q][:], in0=gates[q][:], in1=up_product[:], op=ALU.mult
+                out=results[half][:], in0=gates[half][:], in1=products[UP][half][:], op=ALU.mult
             )
-            nc.sync.dma_start(out=out_rows[:, q * SHARE : (q + 1) * SHARE], in_=results[q][:])
+            nc.sync.dma_start(
+                out=out_rows[:, half * CHUNK : (half + 1) * CHUNK], in_=results[half][:]
+            )
 
-        add_and_square(0)
-        add_and_square(1)
+        add_square_transpose(0)
+        add_square_transpose(1)
         reciprocal_std()
-        take_chunk(0)
-        normalise_transposed(0)
-        normalise_transposed(1)
-        take_chunk(1)
-        take_chunk(2)
         apply_gain(0)
-        take_chunk(3)
         apply_gain(1)
+        regroup_part(nc.vector.tensor_copy, 0, slice(0, CHUNK))
+        regroup(1)
+        quantise(0)
+        normalise(0)
+        normalise(1)
         quantise_n()
-        quantise(3, SCALAR)
+        quantise(1)
         first_contraction(GATE)
-        first_contraction(UP)
+        regroup(2)
+        regroup(3)
+        quantise(2)
         regroup(4)
-        quantise(4, VECTOR)
-        take_chunk(5)
-        regroup(6)
+        quantise(3)
+        first_contraction(UP)
         round_r(GATE)
-        round_r(UP)
-        quantise(5, SCALAR)
+        regroup(5)
         quantise_r(GATE)
-        quantise(6, VECTOR)
+        quantise(4)
+        second_contraction(GATE, 0)
+        regroup(6)
+        quantise(5)
+        second_contraction(GATE, 1)
+        round_r(UP)
+        regroup(7)
         quantise_r(UP)
-        take_chunk(7)
-        for q in range(quarters):
-            gate_quarter(q)
-        quantise(7, SCALAR)
-        for q in range(quarters):
-            finish_quarter(q)
+        quantise(6)
+        second_contraction(UP, 0)
+        silu_gate(0)
+        silu_gate(1)
+        quantise(7)
+        second_contraction(UP, 1)
+        multiply_and_store(0)
+        multiply_and_store(1)

import concourse.mybir as mybir
from concourse.masks import make_identity

BF16 = mybir.dt.bfloat16
F32 = mybir.dt.float32
U32 = mybir.dt.uint32
U8 = mybir.dt.uint8
FP8X4 = mybir.dt.float8_e4m3fn_x4
ALU = mybir.AluOpType
ACT = mybir.ActivationFunctionType

P = 128
PACK = 4
K_PASS = P * PACK
H = 1024
R = 512
I = 1024
PASSES = H // K_PASS
HALVES = I // 512
EPS = 1e-05
CHUNK = 512
RUN = 4
VECTOR_COLS = 256
GATE, UP = 0, 1

FLOPS = 2 * P * (2 * H * R + 2 * R * I)


def tile_neuronllamamlp_pa_s_kernel(
    tc, x, residual, ln_w, w_gate_v, w_gate_u, w_up_v, w_up_u, out
):
    nc = tc.nc
    x_rows = x.flatten_outer_dims()
    res_rows = residual.flatten_outer_dims()
    out_rows = out.flatten_outer_dims()

    with tc.tile_pool(name="keep", bufs=1) as keep, tc.psum_pool(
        name="psum", bufs=1
    ) as psum, tc.manual_schedule():
        x_sb = keep.tile([P, PASSES, K_PASS], BF16, name="x_sb")
        res_sb = keep.tile([P, PASSES, K_PASS], BF16, name="res_sb")
        for g in range(PASSES):
            cols = slice(g * K_PASS, (g + 1) * K_PASS)
            nc.sync.dma_start(out=x_sb[:, g, :], in_=x_rows[:, cols])
            nc.sync.dma_start(out=res_sb[:, g, :], in_=res_rows[:, cols])
        ln_sb = keep.tile([P, PASSES, PACK], BF16, name="ln_sb")
        nc.scalar.dma_start(out=ln_sb[:], in_=ln_w.rearrange("(g p j) -> p g j", p=P, j=PACK))

        chunk_views = []
        for w in (w_gate_v, w_up_v):
            for g in range(PASSES):
                rows = w[g * K_PASS : (g + 1) * K_PASS, :]
                chunk_views.append(rows.rearrange("(p j) r -> p j r", j=PACK))
        for w in (w_gate_u, w_up_u):
            for half in range(HALVES):
                cols = w[:, half * CHUNK : (half + 1) * CHUNK]
                chunk_views.append(cols.rearrange("(j p) i -> p j i", p=P))

        raws, groupeds, codes, scales = [], [], [], []
        for c, view in enumerate(chunk_views):
            raws.append(keep.tile([P, PACK, CHUNK], BF16, name="raw%d" % c))
            groupeds.append(keep.tile([P, CHUNK, PACK], BF16, name="grouped%d" % c, align_bytes=64))
            codes.append(keep.tile([P, CHUNK], U32, name="codes%d" % c, align_bytes=64))
            scales.append(keep.tile([P, CHUNK], U8, name="scales%d" % c, align_bytes=64))
            nc.sync.dma_start(out=raws[c][:], in_=view)

        ident = keep.tile([P, P], F32, name="ident")
        make_identity(nc, ident[:])
        neg_half = keep.tile([P, 1], F32, name="neg_half")
        nc.gpsimd.memset(neg_half[:], -0.5)
        warm_in = keep.tile([P, 1], F32, name="warm_in")
        warm_out = keep.tile([P, 1], F32, name="warm_out")
        nc.vector.memset(warm_in[:], 0.0)
        nc.scalar.activation(out=warm_out[:], in_=warm_in[:], func=ACT.Silu)
        ln_f32 = keep.tile([P, PASSES, PACK], F32, name="ln_f32")
        nc.gpsimd.tensor_copy(out=ln_f32[:], in_=ln_sb[:])

        def regroup_part(copy, c, cols):
            copy(
                out=groupeds[c][:, cols, :].rearrange("p (w i) j -> p w j i", i=RUN),
                in_=raws[c][:, :, cols].rearrange("p j (w i) -> p w j i", i=RUN),
            )

        def regroup(c):
            regroup_part(nc.vector.tensor_copy, c, slice(0, VECTOR_COLS))
            regroup_part(nc.scalar.copy, c, slice(VECTOR_COLS, CHUNK))

        def quantise(c):
            nc.vector.quantize_mx(
                out=codes[c][:].bitcast(FP8X4),
                scales=scales[c][:],
                in_=groupeds[c][:].rearrange("p w j -> p (w j)"),
            )

        h_perm = keep.tile([P, PASSES, PACK, P], F32, name="h_perm")
        squares = keep.tile([P, PASSES, K_PASS], BF16, name="squares")
        mean_parts = keep.tile([P, PASSES], F32, name="mean_parts")
        mean_sq = keep.tile([P, 1], F32, name="mean_sq")
        rstd = keep.tile([P, 1], F32, name="rstd")
        gained = keep.tile([P, PASSES, PACK, P], F32, name="gained")
        n_grouped = keep.tile([P, PASSES, P, PACK], BF16, name="n_grouped", align_bytes=64)
        n_codes = keep.tile([P, PASSES, P], U32, name="n_codes", align_bytes=64)
        n_scales = keep.tile([P, PASSES, P], U8, name="n_scales", align_bytes=64)
        hT = [psum.tile([P, PACK, P], F32, name="hT%d" % g, tag="bank%d" % g) for g in range(PASSES)]
        rstd_rows = psum.tile([P, P], F32, name="rstd_rows", tag="bank2")

        def add_square_transpose(g):
            nc.vector.tensor_tensor(
                out=h_perm[:, g],
                in0=x_sb[:, g, :].rearrange("t (p j) -> t j p", j=PACK),
                in1=res_sb[:, g, :].rearrange("t (p j) -> t j p", j=PACK),
                op=ALU.add,
            )
            nc.scalar.activation(
                out=squares[:, g, :],
                in_=h_perm[:, g].rearrange("t j p -> t (j p)"),
                func=ACT.Square,
                scale=H**-0.5,
                accum_out=mean_parts[:, g : g + 1],
            )
            for j in range(PACK):
                nc.tensor.transpose(hT[g][:, j, :], h_perm[:, g, j, :], ident[:])

        def reciprocal_std():
            nc.gpsimd.tensor_scalar(
                out=mean_sq[:],
                in0=mean_parts[:, 0:1],
                scalar1=mean_parts[:, 1:2],
                scalar2=EPS,
                op0=ALU.add,
                op1=ALU.add,
            )
            nc.gpsimd.tensor_tensor(out=rstd[:], in0=mean_sq[:], in1=neg_half[:], op=ALU.pow)
            nc.tensor.transpose(rstd_rows[:], rstd[:].to_broadcast([P, P]), ident[:])

        def apply_gain(g):
            for j in range(PACK):
                nc.scalar.activation(
                    out=gained[:, g, j, :],
                    in_=hT[g][:, j, :],
                    func=ACT.Copy,
                    scale=ln_f32[:, g, j : j + 1],
                )

        def normalise(g):
            nc.vector.tensor_tensor(
                out=n_grouped[:, g],
                in0=gained[:, g].rearrange("p j t -> p t j"),
                in1=rstd_rows[:].unsqueeze(2).to_broadcast([P, P, PACK]),
                op=ALU.mult,
            )

        def quantise_n():
            nc.vector.quantize_mx(
                out=n_codes[:].rearrange("p g t -> p (g t)").bitcast(FP8X4),
                scales=n_scales[:].rearrange("p g t -> p (g t)"),
                in_=n_grouped[:].rearrange("p g t j -> p (g t j)"),
            )

        rT = [
            psum.tile([P, PACK, P], F32, name="rT%d" % m, tag="bank%d" % (3 + m))
            for m in (GATE, UP)
        ]
        r_grouped = [
            keep.tile([P, P, PACK], BF16, name="r_grouped%d" % m, align_bytes=64)
            for m in (GATE, UP)
        ]
        r_codes = [
            keep.tile([P, P], U32, name="r_codes%d" % m, align_bytes=64) for m in (GATE, UP)
        ]
        r_scales = [
            keep.tile([P, P], U8, name="r_scales%d" % m, align_bytes=64) for m in (GATE, UP)
        ]

        def first_contraction(m):
            for b in range(PACK):
                for g in range(PASSES):
                    c = m * PASSES + g
                    nc.tensor.matmul_mx(
                        out=rT[m][:, b, :],
                        lhsT=codes[c][:, b * P : (b + 1) * P].bitcast(FP8X4),
                        lhsT_scale=scales[c][:, b * P : (b + 1) * P],
                        rhs=n_codes[:, g, :].bitcast(FP8X4),
                        rhs_scale=n_scales[:, g, :],
                        start=(g == 0),
                        stop=(g == PASSES - 1),
                    )

        def round_r(m):
            nc.scalar.copy(out=r_grouped[m][:], in_=rT[m][:].rearrange("p b t -> p t b"))

        def quantise_r(m):
            nc.vector.quantize_mx(
                out=r_codes[m][:].bitcast(FP8X4),
                scales=r_scales[m][:],
                in_=r_grouped[m][:].rearrange("p t b -> p (t b)"),
            )

        products = [
            [
                psum.tile(
                    [P, CHUNK],
                    F32,
                    name="product%d_%d" % (m, half),
                    tag="bank%d" % ((5 + m * HALVES + half) % 8),
                )
                for half in range(HALVES)
            ]
            for m in (GATE, UP)
        ]
        gates = [keep.tile([P, CHUNK], F32, name="gate%d" % half) for half in range(HALVES)]
        results = [keep.tile([P, CHUNK], F32, name="result%d" % half) for half in range(HALVES)]

        def second_contraction(m, half):
            c = 2 * PASSES + m * HALVES + half
            nc.tensor.matmul_mx(
                out=products[m][half][:],
                lhsT=r_codes[m][:].bitcast(FP8X4),
                lhsT_scale=r_scales[m][:],
                rhs=codes[c][:].bitcast(FP8X4),
                rhs_scale=scales[c][:],
                start=True,
                stop=True,
            )

        def silu_gate(half):
            nc.scalar.activation(out=gates[half][:], in_=products[GATE][half][:], func=ACT.Silu)

        def multiply_and_store(half):
            nc.vector.tensor_tensor(
                out=results[half][:], in0=gates[half][:], in1=products[UP][half][:], op=ALU.mult
            )
            nc.sync.dma_start(
                out=out_rows[:, half * CHUNK : (half + 1) * CHUNK], in_=results[half][:]
            )

        add_square_transpose(0)
        add_square_transpose(1)
        reciprocal_std()
        apply_gain(0)
        apply_gain(1)
        regroup_part(nc.vector.tensor_copy, 0, slice(0, CHUNK))
        regroup(1)
        quantise(0)
        normalise(0)
        normalise(1)
        quantise_n()
        quantise(1)
        first_contraction(GATE)
        regroup(2)
        regroup(3)
        quantise(2)
        regroup(4)
        quantise(3)
        first_contraction(UP)
        round_r(GATE)
        regroup(5)
        quantise_r(GATE)
        quantise(4)
        second_contraction(GATE, 0)
        regroup(6)
        quantise(5)
        second_contraction(GATE, 1)
        round_r(UP)
        regroup(7)
        quantise_r(UP)
        quantise(6)
        second_contraction(UP, 0)
        silu_gate(0)
        silu_gate(1)
        quantise(7)
        second_contraction(UP, 1)
        multiply_and_store(0)
        multiply_and_store(1)
